import numpy as np
import ml_dtypes


def mxq(x, axis, fmt="e4m3"):
    dtype, down = {"e4m3": (ml_dtypes.float8_e4m3fn, 7), "e5m2": (ml_dtypes.float8_e5m2, 14)}[fmt]
    v = np.moveaxis(np.asarray(x, np.float32).astype(ml_dtypes.bfloat16).astype(np.float64), axis, -1)
    blocks = v.reshape(v.shape[:-1] + (-1, 32))
    amax = np.abs(blocks).max(-1, keepdims=True)
    byte = np.maximum(np.where(amax > 0, np.frexp(amax)[1] - 1 + 127, 0) - down, 1)
    scale = np.exp2(byte - 127.0)
    codes = (blocks / scale).astype(np.float32).astype(dtype).astype(np.float64)
    return np.moveaxis((codes * scale).reshape(v.shape), -1, axis)


WIDE = False


def mx_kscale(k):
    if not WIDE:
        return np.ones(k)
    levels = np.array([30, -30])
    if k % 512:
        return np.exp2(np.random.permutation(np.resize(levels, k // 32))).repeat(32)
    a = np.empty((k // 512, 16))
    for p in range(k // 512):
        a[p, :8] = np.random.permutation(np.resize(levels, 8))
        for g in range(8):
            far = levels[np.abs(levels - a[p, g]) >= 10]
            a[p, g + 8] = far[np.random.randint(len(far))]
    return np.exp2(a.ravel()).repeat(32)


BF16 = ml_dtypes.bfloat16


def bf(x):
    return np.asarray(x, np.float32).astype(BF16)


def f64(x):
    return np.asarray(x).astype(np.float64)


E2M1 = np.array([0.0, 0.5, 1.0, 1.5, 2.0, 3.0, 4.0, 6.0, -0.0, -0.5, -1.0, -1.5, -2.0, -3.0, -4.0, -6.0])


def pack_weight(w, fmt):
    k, n = w.shape
    w = f64(bf(w)).reshape(k // 32, 32, n)
    amax = np.abs(w).max(1)
    if fmt == "e4m3":
        byte = np.frexp(amax)[1] - 1 + 127 - 7
    else:
        mant, ex = np.frexp(amax / 6.0)
        byte = np.where(mant > 0.5, ex, ex - 1) + 127
    byte = np.clip(np.where(amax > 0, byte, 1), 1, 254)
    scaled = (w * np.exp2(127.0 - byte)[:, None, :]).reshape(k, n).astype(np.float32)
    by_word = np.ascontiguousarray(scaled.reshape(k // 512, 128, 4, n).transpose(0, 1, 3, 2))
    if fmt == "e4m3":
        words = by_word.astype(ml_dtypes.float8_e4m3fn).view(np.uint8)
    else:
        c = by_word.astype(ml_dtypes.float4_e2m1fn).view(np.uint8) & 0xF
        words = c[..., 0::2] | (c[..., 1::2] << 4)
    return np.ascontiguousarray(words), np.ascontiguousarray(byte.astype(np.uint8).reshape(k // 512, 16, n))


def unpack_weight(words, scales, fmt):
    g, p, n, _ = words.shape
    if fmt == "e4m3":
        vals = np.ascontiguousarray(words).view(ml_dtypes.float8_e4m3fn).astype(np.float64)
    else:
        nib = np.empty((g, p, n, 4), np.uint8)
        nib[..., 0::2] = words & 0xF
        nib[..., 1::2] = words >> 4
        vals = E2M1[nib]
    vals = vals * np.repeat(np.exp2(scales.astype(np.float64) - 127.0), 8, axis=1)[..., None]
    return vals.transpose(0, 1, 3, 2).reshape(g * 512, n)

def pack4(w):
    words, scales = pack_weight(w, "e2m1")
    return words.reshape(words.shape[0], 128, -1), scales


def unpack4(words, scales):
    return unpack_weight(words.reshape(words.shape[0], 128, -1, 2), scales, "e2m1")


B, S, D_MODEL, N_HEADS, QK_ROPE, QK_NOPE, KV_LORA, V_DIM = 2, 256, 2048, 16, 128, 128, 512, 128
QK_DIM = QK_ROPE + QK_NOPE
ROPE_BASE = 10000.0


def apply_rope(r):
    freqs = 1.0 / (ROPE_BASE ** (np.arange(0, QK_ROPE, 2) / QK_ROPE))
    t = np.arange(S)[:, None] * freqs[None, :]
    cos = np.cos(t)[None, :, None, :]
    sin = np.sin(t)[None, :, None, :]
    r1 = r[..., 0::2]
    r2 = r[..., 1::2]
    return np.stack([r1 * cos - r2 * sin, r2 * cos + r1 * sin], axis=-1).reshape(r.shape)


def setup_inputs():
    s = mx_kscale(D_MODEL)
    x = bf(np.random.standard_normal((B, S, D_MODEL)) * s)
    words, scales = pack4(np.random.standard_normal((D_MODEL, N_HEADS * QK_DIM)) / np.sqrt(D_MODEL) / s[:, None])
    return {"x": x, "Wq_words": words, "Wq_scales": scales}


def reference(x, Wq_words, Wq_scales):
    q = (mxq(f64(x), 2, "e5m2") @ unpack4(Wq_words, Wq_scales)).reshape(B, S, N_HEADS, QK_DIM)
    q_nope, q_rope = q[..., :QK_NOPE], q[..., QK_NOPE:]
    return np.concatenate([q_nope, apply_rope(q_rope)], axis=-1)

@@ -1,0 +1,216 @@
+import math
+from contextlib import ExitStack
+
+import concourse.mybir as mybir
+from concourse.masks import make_identity
+
+F32 = mybir.dt.float32
+BF16 = mybir.dt.bfloat16
+I32 = mybir.dt.int32
+U32 = mybir.dt.uint32
+U8 = mybir.dt.uint8
+E5M2X4 = mybir.dt.float8_e5m2_x4
+E2M1X4 = mybir.dt.float4_e2m1fn_x4
+ALU = mybir.AluOpType
+ACT = mybir.ActivationFunctionType
+
+P = 128
+TOKENS, K, N = 512, 2048, 4096
+SEQ = 256
+PASSES = K // 512
+TOKEN_TILES = TOKENS // P
+N_TILE = 512
+COL_TILES = N // N_TILE
+ROPE = 128
+FREQ_RATIO = 10000.0 ** (-2.0 / ROPE)
+FLOPS = 2 * TOKENS * K * N
+
+W_GROUPS = [(0, 1), (1, 2), (2, 4), (4, 6), (6, 8)]
+
+
+def tile_multiheadlatentattention_pb_kernel(tc, x, Wq_words, Wq_scales, out):
+    nc = tc.nc
+    x_rows = x.rearrange("b s k -> (b s) k")
+    out_rows = out.rearrange("b s h d -> (b s) (h d)")
+
+    with ExitStack() as ctx:
+        keep = ctx.enter_context(tc.tile_pool(name="keep", bufs=1))
+        work = ctx.enter_context(tc.tile_pool(name="work", bufs=3))
+        outs = ctx.enter_context(tc.tile_pool(name="outs", bufs=12))
+        psum = ctx.enter_context(tc.psum_pool(name="psum", bufs=8))
+        ctx.enter_context(tc.manual_schedule())
+
+        x_sb, grouped, codes, scales, banks = {}, {}, {}, {}, {}
+        w_words, w_scales = {}, {}
+
+        def load_x(t, half):
+            tile = keep.tile([P, K // 2], BF16, name="x_%d_%d" % (t, half))
+            nc.sync.dma_start(out=tile[:], in_=x_rows[P * t : P * (t + 1), (K // 2) * half : (K // 2) * (half + 1)])
+            x_sb[t, half] = tile
+
+        def load_scales(j0, j1):
+            cols = N_TILE * (j1 - j0)
+            plane = keep.tile([P, PASSES, cols], U8, name="ws_%d" % j0, align_bytes=64)
+            for r in range(4):
+                src = Wq_scales[:, r:16:4, N_TILE * j0 : N_TILE * j1].rearrange("g q n -> q g n")
+                nc.sync.dma_start(out=plane[r:P:32, :, :].bitcast(I32), in_=src.bitcast(I32))
+            for j in range(j0, j1):
+                for g in range(PASSES):
+                    w_scales[j, g] = plane[:, g, N_TILE * (j - j0) : N_TILE * (j - j0 + 1)]
+
+        def load_words(j0, j1, g0, g1):
+            cols = N_TILE * (j1 - j0)
+            tile = keep.tile([P, g1 - g0, 2 * cols], U8, name="ww_%d_%d" % (j0, g0), align_bytes=64)
+            src = Wq_words[g0:g1, :, 2 * N_TILE * j0 : 2 * N_TILE * j1].rearrange("g p n -> p g n")
+            nc.sync.dma_start(out=tile[:].bitcast(I32), in_=src.bitcast(I32))
+            for j in range(j0, j1):
+                for g in range(g0, g1):
+                    w_words[j, g] = tile[:, g - g0, 2 * N_TILE * (j - j0) : 2 * N_TILE * (j - j0 + 1)]
+
+        def load_w_group(i):
+            j0, j1 = W_GROUPS[i]
+            load_scales(j0, j1)
+            load_words(j0, j1, 0, PASSES)
+
+        def transpose_x(t, half):
+            bank = psum.tile([P, N_TILE], F32, name="bank")
+            words = x_sb[t, half][:].bitcast(F32)
+            for gl in range(2):
+                for u in range(2):
+                    c = (2 * gl + u) * P
+                    nc.tensor.transpose(bank[:, c : c + P], words[:, 256 * gl + u : 256 * (gl + 1) : 2], ident[:])
+            banks[t, half] = bank
+
+        def copy_out(t, half):
+            tile = keep.tile([P, 2, P, 2], F32, name="grouped_%d_%d" % (t, half), align_bytes=64)
+            nc.scalar.copy(out=tile[:], in_=banks[t, half][:].rearrange("p (g u r) -> p g r u", g=2, u=2))
+            grouped[t, half] = tile
+
+        def quantize(t, half):
+            cd = keep.tile([P, 2 * P], U32, name="codes_%d_%d" % (t, half), align_bytes=64)
+            sc = keep.tile([P, 2 * P], U8, name="xs_%d_%d" % (t, half), align_bytes=64)
+            src = grouped[t, half][:].rearrange("p g r u -> p (g r u)").bitcast(BF16)
+            nc.vector.quantize_mx(out=cd[:].bitcast(E5M2X4), scales=sc[:], in_=src)
+            for gl in range(2):
+                codes[t, 2 * half + gl] = cd[:, P * gl : P * (gl + 1)]
+                scales[t, 2 * half + gl] = sc[:, P * gl : P * (gl + 1)]
+
+        def multiply(t, j):
+            acc = psum.tile([P, N_TILE], F32, name="bank")
+            for g in range(PASSES):
+                nc.tensor.matmul_mx(
+                    out=acc[:],
+                    lhsT=codes[t, g].bitcast(E5M2X4),
+                    lhsT_scale=scales[t, g],
+                    rhs=w_words[j, g].bitcast(E2M1X4),
+                    rhs_scale=w_scales[j, g],
+                    start=(g == 0),
+                    stop=(g == PASSES - 1),
+                )
+            return acc
+
+        pending = []
+
+        def finish():
+            t, j, res, by_cos, by_sin = pending.pop()
+            rope = res[:].rearrange("p (h part i e) -> p h part i e", h=2, part=2, e=2)[:, :, 1, :, :]
+            nc.vector.tensor_tensor(out=rope, in0=by_cos[:], in1=by_sin[:][:, :, :, ::-1], op=ALU.add)
+            nc.sync.dma_start(out=out_rows[P * t : P * (t + 1), N_TILE * j : N_TILE * (j + 1)], in_=res[:])
+
+        def epilogue(t, j, acc):
+            parts = acc[:].rearrange("p (h part d) -> p h part d", h=2, part=2)
+            res = outs.tile([P, N_TILE], F32, name="res")
+            by_cos = work.tile([P, 2, ROPE // 2, 2], F32, name="by_cos")
+            by_sin = work.tile([P, 2, ROPE // 2, 2], F32, name="by_sin")
+            half = t % 2
+            for dst, kind in ((by_sin, 0), (by_cos, 1)):
+                nc.vector.tensor_tensor(
+                    out=dst[:].rearrange("p h i e -> p h (i e)"),
+                    in0=parts[:, :, 1, :],
+                    in1=table[:, kind, half, :].unsqueeze(1).to_broadcast([P, 2, ROPE]),
+                    op=ALU.mult,
+                )
+            nc.scalar.copy(
+                out=res[:].rearrange("p (h part d) -> p h part d", h=2, part=2)[:, :, 0, :], in_=parts[:, :, 0, :]
+            )
+            if pending:
+                finish()
+            pending.append((t, j, res, by_cos, by_sin))
+
+        load_x(0, 0)
+        load_x(0, 1)
+        load_x(1, 0)
+        load_x(1, 1)
+        load_scales(0, 1)
+        load_words(0, 1, 0, 2)
+        load_words(0, 1, 2, 4)
+        for t in (2, 3):
+            load_x(t, 0)
+            load_x(t, 1)
+        load_w_group(1)
+
+        pos = keep.tile([P, 2], I32, name="pos")
+        nc.gpsimd.iota(pos[:], pattern=[[P, 2]], base=0, channel_multiplier=1)
+        ident = keep.tile([P, P], F32, name="ident")
+        make_identity(nc, ident[:])
+        turns = keep.tile([P, 2, ROPE // 2, 2], F32, name="turns")
+        for e, sign in ((0, 1.0), (1, -1.0)):
+            nc.vector.tensor_scalar(
+                out=turns[:, :, 0, e], in0=pos[:], scalar1=sign / (2 * math.pi), scalar2=None, op0=ALU.mult
+            )
+        for n in (1, 4, 16):
+            for m in (1, 2, 3):
+                nc.vector.tensor_scalar(
+                    out=turns[:, :, m * n : (m + 1) * n, :],
+                    in0=turns[:, :, 0:n, :],
+                    scalar1=FREQ_RATIO ** (m * n),
+                    scalar2=None,
+                    op0=ALU.mult,
+                )
+        flat = turns[:].rearrange("p h i e -> p (h i e)")
+        whole = keep.tile([P, 2, 2 * ROPE], I32, name="whole")
+        frac = keep.tile([P, 2, 2 * ROPE], F32, name="frac")
+        for kind in range(2):
+            nc.vector.tensor_scalar(
+                out=whole[:, kind, :], in0=flat, scalar1=0.25 * kind, scalar2=None, op0=ALU.add
+            )
+        for kind in range(2):
+            nc.vector.scalar_tensor_tensor(
+                out=frac[:, kind, :],
+                in0=flat,
+                scalar=0.25 * kind,
+                in1=whole[:, kind, :],
+                op0=ALU.add,
+                op1=ALU.subtract,
+            )
+        table = keep.tile([P, 2, 2, ROPE], F32, name="table")
+
+        for t in (0, 1):
+            for half in range(2):
+                transpose_x(t, half)
+                copy_out(t, half)
+                quantize(t, half)
+        nc.scalar.activation(
+            out=table[:].rearrange("p k h d -> p (k h d)"),
+            in_=frac[:].rearrange("p k n -> p (k n)"),
+            func=ACT.Sin,
+            scale=2 * math.pi,
+        )
+        acc0 = multiply(0, 0)
+        acc1 = multiply(1, 0)
+        for t in (2, 3):
+            for half in range(2):
+                transpose_x(t, half)
+                copy_out(t, half)
+                quantize(t, half)
+        load_w_group(2)
+        epilogue(0, 0, acc0)
+        epilogue(1, 0, acc1)
+        for t in (2, 3):
+            epilogue(t, 0, multiply(t, 0))
+        for j in range(1, COL_TILES):
+            if j in (2, 4):
+                load_w_group(j // 2 + 2)
+            for t in range(TOKEN_TILES):
+                epilogue(t, j, multiply(t, j))
+        finish()

@@ -22,6 +22,7 @@ TOKEN_TILES = TOKENS // P
 N_TILE = 512
 COL_TILES = N // N_TILE
 ROPE = 128
+HEAD = 256
 FREQ_RATIO = 10000.0 ** (-2.0 / ROPE)
 FLOPS = 2 * TOKENS * K * N
 
@@ -95,47 +96,53 @@ def tile_multiheadlatentattention_pb_kernel(tc, x, Wq_words, Wq_scales, out):
                 codes[t, 2 * half + gl] = cd[:, P * gl : P * (gl + 1)]
                 scales[t, 2 * half + gl] = sc[:, P * gl : P * (gl + 1)]
 
-        def multiply(t, j):
+        def multiply(t, h0, heads):
             acc = psum.tile([P, N_TILE], F32, name="bank")
+            j, c0, cols = h0 // 2, HEAD * (h0 % 2), HEAD * heads
             for g in range(PASSES):
                 nc.tensor.matmul_mx(
-                    out=acc[:],
+                    out=acc[:, 0:cols],
                     lhsT=codes[t, g].bitcast(E5M2X4),
                     lhsT_scale=scales[t, g],
-                    rhs=w_words[j, g].bitcast(E2M1X4),
-                    rhs_scale=w_scales[j, g],
+                    rhs=w_words[j, g][:, 2 * c0 : 2 * (c0 + cols)].bitcast(E2M1X4),
+                    rhs_scale=w_scales[j, g][:, c0 : c0 + cols],
                     start=(g == 0),
                     stop=(g == PASSES - 1),
                 )
-            return acc
+            return acc[:, 0:cols].rearrange("p (h part d) -> p h part d", h=heads, part=2)
 
         pending = []
 
         def finish():
-            t, j, res, by_cos, by_sin = pending.pop()
-            rope = res[:].rearrange("p (h part i e) -> p h part i e", h=2, part=2, e=2)[:, :, 1, :, :]
+            t, h0, heads, res, by_cos, by_sin = pending.pop()
+            rope = res[:].rearrange("p h part (i e) -> p h part i e", e=2)[:, :, 1, :, :]
             nc.vector.tensor_tensor(out=rope, in0=by_cos[:], in1=by_sin[:][:, :, :, ::-1], op=ALU.add)
-            nc.sync.dma_start(out=out_rows[P * t : P * (t + 1), N_TILE * j : N_TILE * (j + 1)], in_=res[:])
+            nc.sync.dma_start(
+                out=out_rows[P * t : P * (t + 1), HEAD * h0 : HEAD * (h0 + heads)],
+                in_=res[:].rearrange("p h part d -> p (h part d)"),
+            )
 
-        def epilogue(t, j, acc):
-            parts = acc[:].rearrange("p (h part d) -> p h part d", h=2, part=2)
-            res = outs.tile([P, N_TILE], F32, name="res")
-            by_cos = work.tile([P, 2, ROPE // 2, 2], F32, name="by_cos")
-            by_sin = work.tile([P, 2, ROPE // 2, 2], F32, name="by_sin")
-            half = t % 2
+        def products(t, heads, acc):
+            by_cos = work.tile([P, heads, ROPE // 2, 2], F32, name="by_cos")
+            by_sin = work.tile([P, heads, ROPE // 2, 2], F32, name="by_sin")
             for dst, kind in ((by_sin, 0), (by_cos, 1)):
                 nc.vector.tensor_tensor(
                     out=dst[:].rearrange("p h i e -> p h (i e)"),
-                    in0=parts[:, :, 1, :],
-                    in1=table[:, kind, half, :].unsqueeze(1).to_broadcast([P, 2, ROPE]),
+                    in0=acc[:, :, 1, :],
+                    in1=table[:, kind, t % 2, :].unsqueeze(1).to_broadcast([P, heads, ROPE]),
                     op=ALU.mult,
                 )
-            nc.scalar.copy(
-                out=res[:].rearrange("p (h part d) -> p h part d", h=2, part=2)[:, :, 0, :], in_=parts[:, :, 0, :]
-            )
+            return by_cos, by_sin
+
+        def pass_through(t, h0, heads, acc, prods):
+            res = outs.tile([P, heads, 2, ROPE], F32, name="res")
+            nc.scalar.copy(out=res[:, :, 0, :], in_=acc[:, :, 0, :])
             if pending:
                 finish()
-            pending.append((t, j, res, by_cos, by_sin))
+            pending.append((t, h0, heads, res) + prods)
+
+        def epilogue(t, h0, heads, acc):
+            pass_through(t, h0, heads, acc, products(t, heads, acc))
 
         load_x(0, 0)
         load_x(0, 1)
@@ -196,21 +203,25 @@ def tile_multiheadlatentattention_pb_kernel(tc, x, Wq_words, Wq_scales, out):
             func=ACT.Sin,
             scale=2 * math.pi,
         )
-        acc0 = multiply(0, 0)
-        acc1 = multiply(1, 0)
+        acc0 = multiply(0, 0, 2)
+        acc1 = multiply(1, 0, 2)
+        prods0 = products(0, 2, acc0)
         for t in (2, 3):
             for half in range(2):
                 transpose_x(t, half)
                 copy_out(t, half)
                 quantize(t, half)
         load_w_group(2)
-        epilogue(0, 0, acc0)
-        epilogue(1, 0, acc1)
+        pass_through(0, 0, 2, acc0, prods0)
+        epilogue(1, 0, 2, acc1)
         for t in (2, 3):
-            epilogue(t, 0, multiply(t, 0))
-        for j in range(1, COL_TILES):
+            epilogue(t, 0, 2, multiply(t, 0, 2))
+        for j in range(1, COL_TILES - 1):
             if j in (2, 4):
                 load_w_group(j // 2 + 2)
             for t in range(TOKEN_TILES):
-                epilogue(t, j, multiply(t, j))
+                epilogue(t, 2 * j, 2, multiply(t, 2 * j, 2))
+        for t in range(TOKEN_TILES):
+            for h in (2 * COL_TILES - 2, 2 * COL_TILES - 1):
+                epilogue(t, h, 1, multiply(t, h, 1))
         finish()

@@ -26,7 +26,8 @@ HEAD = 256
 FREQ_RATIO = 10000.0 ** (-2.0 / ROPE)
 FLOPS = 2 * TOKENS * K * N
 
-W_GROUPS = [(0, 1), (1, 2), (2, 4), (4, 6), (6, 8)]
+STORE_GROUPS = [(0, 4), (4, 8), (8, 12), (12, 14), (14, 15), (15, 16)]
+W_GROUPS = [(1, 2), (2, 4), (4, 8)]
 
 
 def tile_multiheadlatentattention_pb_kernel(tc, x, Wq_words, Wq_scales, out):
@@ -37,17 +38,17 @@ def tile_multiheadlatentattention_pb_kernel(tc, x, Wq_words, Wq_scales, out):
     with ExitStack() as ctx:
         keep = ctx.enter_context(tc.tile_pool(name="keep", bufs=1))
         work = ctx.enter_context(tc.tile_pool(name="work", bufs=3))
-        outs = ctx.enter_context(tc.tile_pool(name="outs", bufs=12))
         psum = ctx.enter_context(tc.psum_pool(name="psum", bufs=8))
         ctx.enter_context(tc.manual_schedule())
 
         x_sb, grouped, codes, scales, banks = {}, {}, {}, {}, {}
         w_words, w_scales = {}, {}
 
-        def load_x(t, half):
-            tile = keep.tile([P, K // 2], BF16, name="x_%d_%d" % (t, half))
-            nc.sync.dma_start(out=tile[:], in_=x_rows[P * t : P * (t + 1), (K // 2) * half : (K // 2) * (half + 1)])
-            x_sb[t, half] = tile
+        def load_x(t, half0, half1):
+            tile = keep.tile([P, (K // 2) * (half1 - half0)], BF16, name="x_%d_%d" % (t, half0))
+            nc.sync.dma_start(out=tile[:], in_=x_rows[P * t : P * (t + 1), (K // 2) * half0 : (K // 2) * half1])
+            for half in range(half0, half1):
+                x_sb[t, half] = tile[:, (K // 2) * (half - half0) : (K // 2) * (half - half0 + 1)]
 
         def load_scales(j0, j1):
             cols = N_TILE * (j1 - j0)
@@ -68,14 +69,9 @@ def tile_multiheadlatentattention_pb_kernel(tc, x, Wq_words, Wq_scales, out):
                 for g in range(g0, g1):
                     w_words[j, g] = tile[:, g - g0, 2 * N_TILE * (j - j0) : 2 * N_TILE * (j - j0 + 1)]
 
-        def load_w_group(i):
-            j0, j1 = W_GROUPS[i]
-            load_scales(j0, j1)
-            load_words(j0, j1, 0, PASSES)
-
         def transpose_x(t, half):
             bank = psum.tile([P, N_TILE], F32, name="bank")
-            words = x_sb[t, half][:].bitcast(F32)
+            words = x_sb[t, half].bitcast(F32)
             for gl in range(2):
                 for u in range(2):
                     c = (2 * gl + u) * P
@@ -112,15 +108,23 @@ def tile_multiheadlatentattention_pb_kernel(tc, x, Wq_words, Wq_scales, out):
             return acc[:, 0:cols].rearrange("p (h part d) -> p h part d", h=heads, part=2)
 
         pending = []
+        staged = {}
+        for s0, s1 in STORE_GROUPS:
+            for t in range(TOKEN_TILES):
+                res = keep.tile([P, s1 - s0, 2, ROPE], F32, name="res_%d_%d" % (t, s0))
+                for h in range(s0, s1):
+                    staged[t, h] = (res, s0, s1)
 
         def finish():
-            t, h0, heads, res, by_cos, by_sin = pending.pop()
-            rope = res[:].rearrange("p h part (i e) -> p h part i e", e=2)[:, :, 1, :, :]
+            t, h0, heads, by_cos, by_sin = pending.pop()
+            res, s0, s1 = staged[t, h0]
+            rope = res[:].rearrange("p h part (i e) -> p h part i e", e=2)[:, h0 - s0 : h0 - s0 + heads, 1, :, :]
             nc.vector.tensor_tensor(out=rope, in0=by_cos[:], in1=by_sin[:][:, :, :, ::-1], op=ALU.add)
-            nc.sync.dma_start(
-                out=out_rows[P * t : P * (t + 1), HEAD * h0 : HEAD * (h0 + heads)],
-                in_=res[:].rearrange("p h part d -> p (h part d)"),
-            )
+            if h0 + heads == s1:
+                nc.sync.dma_start(
+                    out=out_rows[P * t : P * (t + 1), HEAD * s0 : HEAD * s1],
+                    in_=res[:].rearrange("p h part d -> p (h part d)"),
+                )
 
         def products(t, heads, acc):
             by_cos = work.tile([P, heads, ROPE // 2, 2], F32, name="by_cos")
@@ -135,26 +139,27 @@ def tile_multiheadlatentattention_pb_kernel(tc, x, Wq_words, Wq_scales, out):
             return by_cos, by_sin
 
         def pass_through(t, h0, heads, acc, prods):
-            res = outs.tile([P, heads, 2, ROPE], F32, name="res")
-            nc.scalar.copy(out=res[:, :, 0, :], in_=acc[:, :, 0, :])
+            res, s0, s1 = staged[t, h0]
+            nc.scalar.copy(out=res[:, h0 - s0 : h0 - s0 + heads, 0, :], in_=acc[:, :, 0, :])
             if pending:
                 finish()
-            pending.append((t, h0, heads, res) + prods)
+            pending.append((t, h0, heads) + prods)
 
         def epilogue(t, h0, heads, acc):
             pass_through(t, h0, heads, acc, products(t, heads, acc))
 
-        load_x(0, 0)
-        load_x(0, 1)
-        load_x(1, 0)
-        load_x(1, 1)
+        load_x(0, 0, 1)
+        load_x(0, 1, 2)
+        load_x(1, 0, 1)
+        load_x(1, 1, 2)
         load_scales(0, 1)
         load_words(0, 1, 0, 2)
         load_words(0, 1, 2, 4)
-        for t in (2, 3):
-            load_x(t, 0)
-            load_x(t, 1)
-        load_w_group(1)
+        load_x(2, 0, 2)
+        load_x(3, 0, 2)
+        for j0, j1 in W_GROUPS:
+            load_scales(j0, j1)
+            load_words(j0, j1, 0, PASSES)
 
         pos = keep.tile([P, 2], I32, name="pos")
         nc.gpsimd.iota(pos[:], pattern=[[P, 2]], base=0, channel_multiplier=1)
@@ -211,17 +216,14 @@ def tile_multiheadlatentattention_pb_kernel(tc, x, Wq_words, Wq_scales, out):
                 transpose_x(t, half)
                 copy_out(t, half)
                 quantize(t, half)
-        load_w_group(2)
         pass_through(0, 0, 2, acc0, prods0)
         epilogue(1, 0, 2, acc1)
         for t in (2, 3):
             epilogue(t, 0, 2, multiply(t, 0, 2))
-        for j in range(1, COL_TILES - 1):
-            if j in (2, 4):
-                load_w_group(j // 2 + 2)
-            for t in range(TOKEN_TILES):
-                epilogue(t, 2 * j, 2, multiply(t, 2 * j, 2))
         for t in range(TOKEN_TILES):
-            for h in (2 * COL_TILES - 2, 2 * COL_TILES - 1):
-                epilogue(t, h, 1, multiply(t, h, 1))
+            epilogue(t, 2, 2, multiply(t, 2, 2))
+        for h0, h1, heads in ((4, 8, 2), (8, 12, 2), (12, 14, 2), (14, 16, 1)):
+            for t in range(TOKEN_TILES):
+                for h in range(h0, h1, heads):
+                    epilogue(t, h, heads, multiply(t, h, heads))
         finish()

import math
from contextlib import ExitStack

import concourse.mybir as mybir
from concourse.masks import make_identity

F32 = mybir.dt.float32
BF16 = mybir.dt.bfloat16
I32 = mybir.dt.int32
U32 = mybir.dt.uint32
U8 = mybir.dt.uint8
E5M2X4 = mybir.dt.float8_e5m2_x4
E2M1X4 = mybir.dt.float4_e2m1fn_x4
ALU = mybir.AluOpType
ACT = mybir.ActivationFunctionType

P = 128
TOKENS, K, N = 512, 2048, 4096
SEQ = 256
PASSES = K // 512
TOKEN_TILES = TOKENS // P
N_TILE = 512
COL_TILES = N // N_TILE
ROPE = 128
HEAD = 256
FREQ_RATIO = 10000.0 ** (-2.0 / ROPE)
FLOPS = 2 * TOKENS * K * N

STORE_GROUPS = [(0, 4), (4, 8), (8, 12), (12, 14), (14, 15), (15, 16)]
W_GROUPS = [(1, 2), (2, 4), (4, 8)]


def tile_multiheadlatentattention_pb_kernel(tc, x, Wq_words, Wq_scales, out):
    nc = tc.nc
    x_rows = x.rearrange("b s k -> (b s) k")
    out_rows = out.rearrange("b s h d -> (b s) (h d)")

    with ExitStack() as ctx:
        keep = ctx.enter_context(tc.tile_pool(name="keep", bufs=1))
        work = ctx.enter_context(tc.tile_pool(name="work", bufs=3))
        psum = ctx.enter_context(tc.psum_pool(name="psum", bufs=8))
        ctx.enter_context(tc.manual_schedule())

        x_sb, grouped, codes, scales, banks = {}, {}, {}, {}, {}
        w_words, w_scales = {}, {}

        def load_x(t, half0, half1):
            tile = keep.tile([P, (K // 2) * (half1 - half0)], BF16, name="x_%d_%d" % (t, half0))
            nc.sync.dma_start(out=tile[:], in_=x_rows[P * t : P * (t + 1), (K // 2) * half0 : (K // 2) * half1])
            for half in range(half0, half1):
                x_sb[t, half] = tile[:, (K // 2) * (half - half0) : (K // 2) * (half - half0 + 1)]

        def load_scales(j0, j1):
            cols = N_TILE * (j1 - j0)
            plane = keep.tile([P, PASSES, cols], U8, name="ws_%d" % j0, align_bytes=64)
            for r in range(4):
                src = Wq_scales[:, r:16:4, N_TILE * j0 : N_TILE * j1].rearrange("g q n -> q g n")
                nc.sync.dma_start(out=plane[r:P:32, :, :].bitcast(I32), in_=src.bitcast(I32))
            for j in range(j0, j1):
                for g in range(PASSES):
                    w_scales[j, g] = plane[:, g, N_TILE * (j - j0) : N_TILE * (j - j0 + 1)]

        def load_words(j0, j1, g0, g1):
            cols = N_TILE * (j1 - j0)
            tile = keep.tile([P, g1 - g0, 2 * cols], U8, name="ww_%d_%d" % (j0, g0), align_bytes=64)
            src = Wq_words[g0:g1, :, 2 * N_TILE * j0 : 2 * N_TILE * j1].rearrange("g p n -> p g n")
            nc.sync.dma_start(out=tile[:].bitcast(I32), in_=src.bitcast(I32))
            for j in range(j0, j1):
                for g in range(g0, g1):
                    w_words[j, g] = tile[:, g - g0, 2 * N_TILE * (j - j0) : 2 * N_TILE * (j - j0 + 1)]

        def transpose_x(t, half):
            bank = psum.tile([P, N_TILE], F32, name="bank")
            words = x_sb[t, half].bitcast(F32)
            for gl in range(2):
                for u in range(2):
                    c = (2 * gl + u) * P
                    nc.tensor.transpose(bank[:, c : c + P], words[:, 256 * gl + u : 256 * (gl + 1) : 2], ident[:])
            banks[t, half] = bank

        def copy_out(t, half):
            tile = keep.tile([P, 2, P, 2], F32, name="grouped_%d_%d" % (t, half), align_bytes=64)
            nc.scalar.copy(out=tile[:], in_=banks[t, half][:].rearrange("p (g u r) -> p g r u", g=2, u=2))
            grouped[t, half] = tile

        def quantize(t, half):
            cd = keep.tile([P, 2 * P], U32, name="codes_%d_%d" % (t, half), align_bytes=64)
            sc = keep.tile([P, 2 * P], U8, name="xs_%d_%d" % (t, half), align_bytes=64)
            src = grouped[t, half][:].rearrange("p g r u -> p (g r u)").bitcast(BF16)
            nc.vector.quantize_mx(out=cd[:].bitcast(E5M2X4), scales=sc[:], in_=src)
            for gl in range(2):
                codes[t, 2 * half + gl] = cd[:, P * gl : P * (gl + 1)]
                scales[t, 2 * half + gl] = sc[:, P * gl : P * (gl + 1)]

        def multiply(t, h0, heads):
            acc = psum.tile([P, N_TILE], F32, name="bank")
            j, c0, cols = h0 // 2, HEAD * (h0 % 2), HEAD * heads
            for g in range(PASSES):
                nc.tensor.matmul_mx(
                    out=acc[:, 0:cols],
                    lhsT=codes[t, g].bitcast(E5M2X4),
                    lhsT_scale=scales[t, g],
                    rhs=w_words[j, g][:, 2 * c0 : 2 * (c0 + cols)].bitcast(E2M1X4),
                    rhs_scale=w_scales[j, g][:, c0 : c0 + cols],
                    start=(g == 0),
                    stop=(g == PASSES - 1),
                )
            return acc[:, 0:cols].rearrange("p (h part d) -> p h part d", h=heads, part=2)

        pending = []
        staged = {}
        for s0, s1 in STORE_GROUPS:
            for t in range(TOKEN_TILES):
                res = keep.tile([P, s1 - s0, 2, ROPE], F32, name="res_%d_%d" % (t, s0))
                for h in range(s0, s1):
                    staged[t, h] = (res, s0, s1)

        def finish():
            t, h0, heads, by_cos, by_sin = pending.pop()
            res, s0, s1 = staged[t, h0]
            rope = res[:].rearrange("p h part (i e) -> p h part i e", e=2)[:, h0 - s0 : h0 - s0 + heads, 1, :, :]
            nc.vector.tensor_tensor(out=rope, in0=by_cos[:], in1=by_sin[:][:, :, :, ::-1], op=ALU.add)
            if h0 + heads == s1:
                nc.sync.dma_start(
                    out=out_rows[P * t : P * (t + 1), HEAD * s0 : HEAD * s1],
                    in_=res[:].rearrange("p h part d -> p (h part d)"),
                )

        def products(t, heads, acc):
            by_cos = work.tile([P, heads, ROPE // 2, 2], F32, name="by_cos")
            by_sin = work.tile([P, heads, ROPE // 2, 2], F32, name="by_sin")
            for dst, kind in ((by_sin, 0), (by_cos, 1)):
                nc.vector.tensor_tensor(
                    out=dst[:].rearrange("p h i e -> p h (i e)"),
                    in0=acc[:, :, 1, :],
                    in1=table[:, kind, t % 2, :].unsqueeze(1).to_broadcast([P, heads, ROPE]),
                    op=ALU.mult,
                )
            return by_cos, by_sin

        def pass_through(t, h0, heads, acc, prods):
            res, s0, s1 = staged[t, h0]
            nc.scalar.copy(out=res[:, h0 - s0 : h0 - s0 + heads, 0, :], in_=acc[:, :, 0, :])
            if pending:
                finish()
            pending.append((t, h0, heads) + prods)

        def epilogue(t, h0, heads, acc):
            pass_through(t, h0, heads, acc, products(t, heads, acc))

        load_x(0, 0, 1)
        load_x(0, 1, 2)
        load_x(1, 0, 1)
        load_x(1, 1, 2)
        load_scales(0, 1)
        load_words(0, 1, 0, 2)
        load_words(0, 1, 2, 4)
        load_x(2, 0, 2)
        load_x(3, 0, 2)
        for j0, j1 in W_GROUPS:
            load_scales(j0, j1)
            load_words(j0, j1, 0, PASSES)

        pos = keep.tile([P, 2], I32, name="pos")
        nc.gpsimd.iota(pos[:], pattern=[[P, 2]], base=0, channel_multiplier=1)
        ident = keep.tile([P, P], F32, name="ident")
        make_identity(nc, ident[:])
        turns = keep.tile([P, 2, ROPE // 2, 2], F32, name="turns")
        for e, sign in ((0, 1.0), (1, -1.0)):
            nc.vector.tensor_scalar(
                out=turns[:, :, 0, e], in0=pos[:], scalar1=sign / (2 * math.pi), scalar2=None, op0=ALU.mult
            )
        for n in (1, 4, 16):
            for m in (1, 2, 3):
                nc.vector.tensor_scalar(
                    out=turns[:, :, m * n : (m + 1) * n, :],
                    in0=turns[:, :, 0:n, :],
                    scalar1=FREQ_RATIO ** (m * n),
                    scalar2=None,
                    op0=ALU.mult,
                )
        flat = turns[:].rearrange("p h i e -> p (h i e)")
        whole = keep.tile([P, 2, 2 * ROPE], I32, name="whole")
        frac = keep.tile([P, 2, 2 * ROPE], F32, name="frac")
        for kind in range(2):
            nc.vector.tensor_scalar(
                out=whole[:, kind, :], in0=flat, scalar1=0.25 * kind, scalar2=None, op0=ALU.add
            )
        for kind in range(2):
            nc.vector.scalar_tensor_tensor(
                out=frac[:, kind, :],
                in0=flat,
                scalar=0.25 * kind,
                in1=whole[:, kind, :],
                op0=ALU.add,
                op1=ALU.subtract,
            )
        table = keep.tile([P, 2, 2, ROPE], F32, name="table")

        for t in (0, 1):
            for half in range(2):
                transpose_x(t, half)
                copy_out(t, half)
                quantize(t, half)
        nc.scalar.activation(
            out=table[:].rearrange("p k h d -> p (k h d)"),
            in_=frac[:].rearrange("p k n -> p (k n)"),
            func=ACT.Sin,
            scale=2 * math.pi,
        )
        acc0 = multiply(0, 0, 2)
        acc1 = multiply(1, 0, 2)
        prods0 = products(0, 2, acc0)
        for t in (2, 3):
            for half in range(2):
                transpose_x(t, half)
                copy_out(t, half)
                quantize(t, half)
        pass_through(0, 0, 2, acc0, prods0)
        epilogue(1, 0, 2, acc1)
        for t in (2, 3):
            epilogue(t, 0, 2, multiply(t, 0, 2))
        for t in range(TOKEN_TILES):
            epilogue(t, 2, 2, multiply(t, 2, 2))
        for h0, h1, heads in ((4, 8, 2), (8, 12, 2), (12, 14, 2), (14, 16, 1)):
            for t in range(TOKEN_TILES):
                for h in range(h0, h1, heads):
                    epilogue(t, h, heads, multiply(t, h, heads))
        finish()
